import numpy as np
import ml_dtypes


def mxq(x, axis, fmt="e4m3"):
    dtype, down = {"e4m3": (ml_dtypes.float8_e4m3fn, 7), "e5m2": (ml_dtypes.float8_e5m2, 14)}[fmt]
    v = np.moveaxis(np.asarray(x, np.float32).astype(ml_dtypes.bfloat16).astype(np.float64), axis, -1)
    blocks = v.reshape(v.shape[:-1] + (-1, 32))
    amax = np.abs(blocks).max(-1, keepdims=True)
    byte = np.maximum(np.where(amax > 0, np.frexp(amax)[1] - 1 + 127, 0) - down, 1)
    scale = np.exp2(byte - 127.0)
    codes = (blocks / scale).astype(np.float32).astype(dtype).astype(np.float64)
    return np.moveaxis((codes * scale).reshape(v.shape), -1, axis)


WIDE = False


def mx_kscale(k):
    if not WIDE:
        return np.ones(k)
    levels = np.array([10, -10, 5, -5, 0])
    a = np.random.permutation(np.resize(levels, k // 512 * 4)).reshape(k // 512, 4)
    idx = np.arange(k)
    return np.exp2(a[idx // 512, idx % 128 // 32])


BF16 = ml_dtypes.bfloat16


def bf(x):
    return np.asarray(x, np.float32).astype(BF16)


def f64(x):
    return np.asarray(x).astype(np.float64)


E2M1 = np.array([0.0, 0.5, 1.0, 1.5, 2.0, 3.0, 4.0, 6.0, -0.0, -0.5, -1.0, -1.5, -2.0, -3.0, -4.0, -6.0])


def pack_weight(w, fmt):
    k, n = w.shape
    w = f64(bf(w)).reshape(k // 32, 32, n)
    amax = np.abs(w).max(1)
    if fmt == "e4m3":
        byte = np.frexp(amax)[1] - 1 + 127 - 7
    else:
        mant, ex = np.frexp(amax / 6.0)
        byte = np.where(mant > 0.5, ex, ex - 1) + 127
    byte = np.clip(np.where(amax > 0, byte, 1), 1, 254)
    scaled = (w * np.exp2(127.0 - byte)[:, None, :]).reshape(k, n).astype(np.float32)
    by_word = np.ascontiguousarray(scaled.reshape(k // 512, 128, 4, n).transpose(0, 1, 3, 2))
    if fmt == "e4m3":
        words = by_word.astype(ml_dtypes.float8_e4m3fn).view(np.uint8)
    else:
        c = by_word.astype(ml_dtypes.float4_e2m1fn).view(np.uint8) & 0xF
        words = c[..., 0::2] | (c[..., 1::2] << 4)
    return np.ascontiguousarray(words), np.ascontiguousarray(byte.astype(np.uint8).reshape(k // 512, 16, n))


def unpack_weight(words, scales, fmt):
    g, p, n, _ = words.shape
    if fmt == "e4m3":
        vals = np.ascontiguousarray(words).view(ml_dtypes.float8_e4m3fn).astype(np.float64)
    else:
        nib = np.empty((g, p, n, 4), np.uint8)
        nib[..., 0::2] = words & 0xF
        nib[..., 1::2] = words >> 4
        vals = E2M1[nib]
    vals = vals * np.repeat(np.exp2(scales.astype(np.float64) - 127.0), 8, axis=1)[..., None]
    return vals.transpose(0, 1, 3, 2).reshape(g * 512, n)


B, D, L = 512, 2048, 4
FMT = "e4m3"


def relu(v):
    return np.maximum(v, 0.0)


def setup_inputs():
    s = mx_kscale(D)
    h_prev = bf(relu(np.random.standard_normal((B, D))) * s)
    x = bf(np.random.standard_normal((B, D)) * 1.5 / np.sqrt(np.sqrt(D)))
    w_last = np.random.standard_normal((D, D)) * 2.0 / np.sqrt(D) / s[None, :]
    b_last = bf(np.random.standard_normal(D) * 0.2)
    w_out = np.random.standard_normal((D, D)) / np.sqrt(D)
    b_out = bf(np.random.standard_normal(D) * 0.2)
    w_last_words, w_last_scales = pack_weight(np.ascontiguousarray(w_last.T), FMT)
    w_out_words, w_out_scales = pack_weight(np.ascontiguousarray(w_out.T), FMT)
    return {"h_prev": h_prev,
            "x": x,
            "w_last_words": w_last_words,
            "w_last_scales": w_last_scales,
            "b_last": b_last,
            "w_out_words": w_out_words,
            "w_out_scales": w_out_scales,
            "b_out": b_out}


def reference(h_prev, x, w_last_words, w_last_scales, b_last, w_out_words, w_out_scales, b_out):
    xf = f64(x)
    interactions = relu(xf * xf.sum(axis=1, keepdims=True))
    h = relu((mxq(f64(h_prev), 1, "e4m3") @ unpack_weight(w_last_words, w_last_scales, FMT)) + f64(b_last))
    z = (h + interactions) * 0.5
    return (mxq(z, 1, "e4m3") @ unpack_weight(w_out_words, w_out_scales, FMT)) + f64(b_out)

@@ -1,0 +1,255 @@
+from contextlib import ExitStack
+
+import concourse.mybir as mybir
+from concourse.masks import make_identity
+
+F32 = mybir.dt.float32
+BF16 = mybir.dt.bfloat16
+I32 = mybir.dt.int32
+U32 = mybir.dt.uint32
+U8 = mybir.dt.uint8
+FP8X4 = mybir.dt.float8_e4m3fn_x4
+ALU = mybir.AluOpType
+ACT = mybir.ActivationFunctionType
+
+P = 128
+PACK = 4
+K_PASS = P * PACK
+ROWS = 512
+FEATURES = 2048
+ROW_TILES = ROWS // P
+PASSES = FEATURES // K_PASS
+BANK = 512
+CHUNKS = FEATURES // BANK
+PAIR = 2
+
+FLOPS = 2 * 2 * ROWS * FEATURES * FEATURES
+
+
+def tile_deepfm_pa_kernel(
+    tc, h_prev, x, w_last_words, w_last_scales, b_last, w_out_words, w_out_scales, b_out, out
+):
+    nc = tc.nc
+    with ExitStack() as ctx:
+        keep = ctx.enter_context(tc.tile_pool(name="keep", bufs=1))
+        rows_pool = ctx.enter_context(tc.tile_pool(name="rows", bufs=ROW_TILES))
+        wide_pool = ctx.enter_context(tc.tile_pool(name="wide", bufs=ROW_TILES))
+        sums_pool = ctx.enter_context(tc.tile_pool(name="sums", bufs=12))
+        stage = ctx.enter_context(tc.tile_pool(name="stage", bufs=2))
+        results = ctx.enter_context(tc.tile_pool(name="results", bufs=4))
+        psum = ctx.enter_context(tc.psum_pool(name="psum", bufs=8))
+
+        ident_f32 = keep.tile([P, P], F32)
+        make_identity(nc, ident_f32[:])
+        ident_bf16 = keep.tile([P, P], BF16)
+        make_identity(nc, ident_bf16[:])
+        ones = keep.tile([P, P], BF16)
+        nc.vector.memset(ones[:], 1.0)
+
+        planes = keep.tile([P, 2, FEATURES], U8, align_bytes=64)
+        nc.vector.memset(planes[:].rearrange("p w n -> p (w n)").bitcast(I32), 0)
+
+        bias_rows = wide_pool.tile([P, 2, FEATURES], BF16, tag="wide")
+        nc.vector.memset(bias_rows[:], 0.0)
+        nc.scalar.dma_start(out=bias_rows[0:1, 0, :], in_=b_last.unsqueeze(0))
+        nc.scalar.dma_start(out=bias_rows[0:1, 1, :], in_=b_out.unsqueeze(0))
+
+        def load_rows(source, b, name):
+            tile_ = rows_pool.tile([P, FEATURES], BF16, name=name, tag=name)
+            nc.sync.dma_start(out=tile_[:], in_=source[b * P : (b + 1) * P, :])
+            return tile_
+
+        def load_planes(w, scales):
+            for q in range(4):
+                nc.sync.dma_start(
+                    out=planes[32 * q : 32 * q + 16, w, :].bitcast(I32),
+                    in_=scales[:, 4 * q : 4 * q + 4, :].bitcast(I32),
+                )
+
+        def load_chunk(words, c, name):
+            chunk = keep.tile([P, PASSES, BANK], U32, name=name, align_bytes=64)
+            source = words.rearrange("g p n t -> p g (n t)")[:, :, PACK * BANK * c : PACK * BANK * (c + 1)]
+            nc.sync.dma_start(out=chunk[:].bitcast(I32), in_=source.bitcast(I32))
+            return chunk
+
+        h_rows = [load_rows(h_prev, b, "h_rows") for b in range(ROW_TILES)]
+        load_planes(0, w_last_scales)
+        w_last = [load_chunk(w_last_words, c, "w_last_%d" % c) for c in range(2)]
+        x_rows = [load_rows(x, b, "x_rows") for b in range(2)]
+        w_last += [load_chunk(w_last_words, c, "w_last_%d" % c) for c in range(2, CHUNKS)]
+        x_rows += [load_rows(x, b, "x_rows") for b in range(2, ROW_TILES)]
+        load_planes(1, w_out_scales)
+        w_out = [load_chunk(w_out_words, c, "w_out_%d" % c) for c in range(CHUNKS)]
+
+        h_words = keep.tile([P, ROW_TILES, PASSES, P], U32, align_bytes=64)
+        h_scales = keep.tile([P, ROW_TILES, PASSES, P], U8, align_bytes=64)
+        for b in range(ROW_TILES):
+            grouped = stage.tile([P, PASSES, P, PACK], BF16, name="grouped_h", align_bytes=64)
+            pairs = h_rows[b][:].bitcast(F32)
+            for gp in range(PASSES // 2):
+                turned = psum.tile([P, 2, 2, P], F32, name="turned_h", tag="bank")
+                for gl in range(2):
+                    g = 2 * gp + gl
+                    for u in range(2):
+                        nc.tensor.transpose(
+                            turned[:, gl, u, :], pairs[:, 256 * g + u : 256 * (g + 1) : 2], ident_f32[:]
+                        )
+                nc.scalar.copy(
+                    out=grouped[:, 2 * gp : 2 * gp + 2, :, :].bitcast(F32),
+                    in_=turned[:].rearrange("p g u r -> p g r u"),
+                )
+            nc.vector.quantize_mx(
+                out=h_words[:, b, :, :].rearrange("p g r -> p (g r)").bitcast(FP8X4),
+                scales=h_scales[:, b, :, :].rearrange("p g r -> p (g r)"),
+                in_=grouped[:].rearrange("p g r t -> p (g r t)"),
+            )
+
+        half_b_last = keep.tile([P, FEATURES], BF16)
+        b_out_all = keep.tile([P, FEATURES], BF16)
+        for w, (target, factor) in enumerate(((half_b_last, 0.5), (b_out_all, 1.0))):
+            for i in range(FEATURES // (2 * BANK)):
+                spread = psum.tile([P, 2 * BANK], BF16, name="spread", tag="bank")
+                for j in range(2):
+                    nc.tensor.matmul(
+                        out=spread[:, j * BANK : (j + 1) * BANK],
+                        lhsT=ones[:],
+                        rhs=bias_rows[:, w, (2 * i + j) * BANK : (2 * i + j + 1) * BANK],
+                        start=True,
+                        stop=True,
+                    )
+                nc.scalar.mul(target[:, 2 * i * BANK : 2 * (i + 1) * BANK], spread[:], factor)
+
+        half_inter = {}
+        half_sums = {}
+        z_rows = {}
+        z_words = keep.tile([P, PAIR, PASSES, PAIR * P], U32, align_bytes=64)
+        z_scales = keep.tile([P, PAIR, PASSES, PAIR * P], U8, align_bytes=64)
+
+        def interactions(b):
+            half_sum = keep.tile([P, 1], F32, name="half_sum_%d" % b)
+            half_inter[b] = wide_pool.tile([P, FEATURES], F32, name="half_inter", tag="wide")
+            nc.scalar.activation(
+                out=half_inter[b][:], in_=x_rows[b][:], func=ACT.Copy, scale=0.5, accum_out=half_sum[:]
+            )
+            if b < PAIR:
+                nc.vector.tensor_scalar(
+                    out=half_inter[b][:],
+                    in0=x_rows[b][:],
+                    scalar1=half_sum[:, 0:1],
+                    scalar2=0.0,
+                    op0=ALU.mult,
+                    op1=ALU.max,
+                )
+            else:
+                nc.scalar.activation(out=half_inter[b][:], in_=x_rows[b][:], func=ACT.Relu, scale=half_sum[:, 0:1])
+
+        def finish_z(b, c):
+            if b not in z_rows:
+                z_rows[b] = rows_pool.tile([P, CHUNKS, PACK, P], BF16, name="z_rows", tag="h_rows")
+            nc.vector.scalar_tensor_tensor(
+                out=z_rows[b][:, c, :, :],
+                in0=half_sums[(b, c)][:].rearrange("r (p t) -> r t p", t=PACK),
+                scalar=0.0,
+                in1=half_inter[b][:, c * BANK : (c + 1) * BANK].rearrange("r (p t) -> r t p", t=PACK),
+                op0=ALU.max,
+                op1=ALU.add,
+            )
+
+        def unit_banks(half, pair):
+            return [(PAIR * half + bl, PAIR * pair + cl) for bl in range(PAIR) for cl in range(PAIR)]
+
+        def first_layer(half, pair, owed):
+            for i, (b, c) in enumerate(unit_banks(half, pair)):
+                acc = psum.tile([P, BANK], F32, name="acc", tag="bank")
+                for g in range(PASSES):
+                    nc.tensor.matmul_mx(
+                        out=acc[:],
+                        lhsT=h_words[:, b, g, :].bitcast(FP8X4),
+                        lhsT_scale=h_scales[:, b, g, :],
+                        rhs=w_last[c][:, g, :].bitcast(FP8X4),
+                        rhs_scale=planes[4 * g : P, 0, c * BANK : (c + 1) * BANK],
+                        start=(g == 0),
+                        stop=(g == PASSES - 1),
+                    )
+                half_sums[(b, c)] = sums_pool.tile([P, BANK], F32, name="half_sums")
+                nc.vector.scalar_tensor_tensor(
+                    out=half_sums[(b, c)][:],
+                    in0=acc[:],
+                    scalar=0.5,
+                    in1=half_b_last[:, c * BANK : (c + 1) * BANK],
+                    op0=ALU.mult,
+                    op1=ALU.add,
+                )
+                if owed:
+                    finish_z(*owed[i])
+
+        def quantise_z(half, pair):
+            grouped = stage.tile([P, PAIR, PAIR * P, PACK], BF16, name="grouped_z", align_bytes=64)
+            for cl in range(PAIR):
+                turned = psum.tile([P, PAIR, PACK, P], BF16, name="turned_z", tag="bank")
+                for bl in range(PAIR):
+                    for t in range(PACK):
+                        nc.tensor.transpose(
+                            turned[:, bl, t, :], z_rows[PAIR * half + bl][:, PAIR * pair + cl, t, :], ident_bf16[:]
+                        )
+                nc.scalar.copy(
+                    out=grouped[:, cl, :, :].rearrange("p (b r) t -> p b r t", b=PAIR),
+                    in_=turned[:].rearrange("p b t r -> p b r t"),
+                )
+            nc.vector.quantize_mx(
+                out=z_words[:, half, PAIR * pair : PAIR * (pair + 1), :].rearrange("p g r -> p (g r)").bitcast(FP8X4),
+                scales=z_scales[:, half, PAIR * pair : PAIR * (pair + 1), :].rearrange("p g r -> p (g r)"),
+                in_=grouped[:].rearrange("p g r t -> p (g r t)"),
+            )
+
+        def second_layer(half, pair, owed):
+            banks = unit_banks(half, pair)
+            accs = {}
+            for bank in banks:
+                accs[bank] = psum.tile([P, BANK], F32, name="acc", tag="bank")
+            for piece in range(PAIR):
+                for b, c in banks:
+                    for g in range(PAIR * piece, PAIR * (piece + 1)):
+                        bl = b - PAIR * half
+                        nc.tensor.matmul_mx(
+                            out=accs[(b, c)][:],
+                            lhsT=z_words[:, half, g, bl * P : (bl + 1) * P].bitcast(FP8X4),
+                            lhsT_scale=z_scales[:, half, g, bl * P : (bl + 1) * P],
+                            rhs=w_out[c][:, g, :].bitcast(FP8X4),
+                            rhs_scale=planes[4 * g : P, 1, c * BANK : (c + 1) * BANK],
+                            start=(g == 0),
+                            stop=(g == PASSES - 1),
+                        )
+            for bl in range(PAIR):
+                b = PAIR * half + bl
+                result = results.tile([P, PAIR * BANK], F32, name="result")
+                for cl in range(PAIR):
+                    c = PAIR * pair + cl
+                    nc.vector.tensor_tensor(
+                        out=result[:, cl * BANK : (cl + 1) * BANK],
+                        in0=accs[(b, c)][:],
+                        in1=b_out_all[:, c * BANK : (c + 1) * BANK],
+                        op=ALU.add,
+                    )
+                    if owed:
+                        finish_z(*owed[PAIR * bl + cl])
+                nc.sync.dma_start(
+                    out=out[b * P : (b + 1) * P, PAIR * pair * BANK : PAIR * (pair + 1) * BANK], in_=result[:]
+                )
+
+        first_layer(0, 0, [])
+        first_layer(1, 0, [])
+        interactions(0)
+        interactions(1)
+        first_layer(0, 1, unit_banks(0, 0))
+        quantise_z(0, 0)
+        interactions(2)
+        interactions(3)
+        first_layer(1, 1, unit_banks(0, 1))
+        quantise_z(0, 1)
+        second_layer(0, 0, unit_banks(1, 0))
+        quantise_z(1, 0)
+        second_layer(0, 1, unit_banks(1, 1))
+        quantise_z(1, 1)
+        second_layer(1, 0, [])
+        second_layer(1, 1, [])

@@ -147,10 +147,10 @@ def tile_deepfm_pa_kernel(
             if b not in z_rows:
                 z_rows[b] = rows_pool.tile([P, CHUNKS, PACK, P], BF16, name="z_rows", tag="h_rows")
             nc.vector.scalar_tensor_tensor(
-                out=z_rows[b][:, c, :, :],
-                in0=half_sums[(b, c)][:].rearrange("r (p t) -> r t p", t=PACK),
+                out=z_rows[b][:, c, :, :].rearrange("r t p -> r p t"),
+                in0=half_sums[(b, c)][:].rearrange("r (p t) -> r p t", t=PACK),
                 scalar=0.0,
-                in1=half_inter[b][:, c * BANK : (c + 1) * BANK].rearrange("r (p t) -> r t p", t=PACK),
+                in1=half_inter[b][:, c * BANK : (c + 1) * BANK].rearrange("r (p t) -> r p t", t=PACK),
                 op0=ALU.max,
                 op1=ALU.add,
             )

@@ -34,222 +34,342 @@ def tile_deepfm_pa_kernel(
         keep = ctx.enter_context(tc.tile_pool(name="keep", bufs=1))
         rows_pool = ctx.enter_context(tc.tile_pool(name="rows", bufs=ROW_TILES))
         wide_pool = ctx.enter_context(tc.tile_pool(name="wide", bufs=ROW_TILES))
-        sums_pool = ctx.enter_context(tc.tile_pool(name="sums", bufs=12))
-        stage = ctx.enter_context(tc.tile_pool(name="stage", bufs=2))
+        sums_pool = ctx.enter_context(tc.tile_pool(name="sums", bufs=10))
+        stage = ctx.enter_context(tc.tile_pool(name="stage", bufs=3))
         results = ctx.enter_context(tc.tile_pool(name="results", bufs=4))
         psum = ctx.enter_context(tc.psum_pool(name="psum", bufs=8))
+        ctx.enter_context(tc.manual_schedule())
 
-        ident_f32 = keep.tile([P, P], F32)
-        make_identity(nc, ident_f32[:])
+        bias_rows = keep.tile([P, BANK], BF16)
+        nc.vector.memset(bias_rows[:].bitcast(I32), 0)
+        nc.scalar.dma_start(out=bias_rows[0:CHUNKS, :], in_=b_last.rearrange("(c n) -> c n", c=CHUNKS))
+        nc.scalar.dma_start(out=bias_rows[CHUNKS : 2 * CHUNKS, :], in_=b_out.rearrange("(c n) -> c n", c=CHUNKS))
+
+        planes_last = keep.tile([P, FEATURES], U8, align_bytes=64)
+        planes_out = keep.tile([P, FEATURES], U8, align_bytes=64)
+        nc.vector.memset(planes_last[:].bitcast(I32), 0)
+        nc.vector.memset(planes_out[:].bitcast(I32), 0)
+
         ident_bf16 = keep.tile([P, P], BF16)
         make_identity(nc, ident_bf16[:])
-        ones = keep.tile([P, P], BF16)
-        nc.vector.memset(ones[:], 1.0)
-
-        planes = keep.tile([P, 2, FEATURES], U8, align_bytes=64)
-        nc.vector.memset(planes[:].rearrange("p w n -> p (w n)").bitcast(I32), 0)
-
-        bias_rows = wide_pool.tile([P, 2, FEATURES], BF16, tag="wide")
-        nc.vector.memset(bias_rows[:], 0.0)
-        nc.scalar.dma_start(out=bias_rows[0:1, 0, :], in_=b_last.unsqueeze(0))
-        nc.scalar.dma_start(out=bias_rows[0:1, 1, :], in_=b_out.unsqueeze(0))
+        ident_f32 = keep.tile([P, P], F32)
+        make_identity(nc, ident_f32[:])
 
         def load_rows(source, b, name):
             tile_ = rows_pool.tile([P, FEATURES], BF16, name=name, tag=name)
             nc.sync.dma_start(out=tile_[:], in_=source[b * P : (b + 1) * P, :])
             return tile_
 
-        def load_planes(w, scales):
+        def load_planes(planes, scales):
             for q in range(4):
                 nc.sync.dma_start(
-                    out=planes[32 * q : 32 * q + 16, w, :].bitcast(I32),
+                    out=planes[32 * q : 32 * q + 16, :].bitcast(I32),
                     in_=scales[:, 4 * q : 4 * q + 4, :].bitcast(I32),
                 )
 
-        def load_chunk(words, c, name):
-            chunk = keep.tile([P, PASSES, BANK], U32, name=name, align_bytes=64)
-            source = words.rearrange("g p n t -> p g (n t)")[:, :, PACK * BANK * c : PACK * BANK * (c + 1)]
+        def load_chunk_half(words, c, half, name):
+            g0 = half * PAIR
+            chunk = keep.tile([P, PAIR, BANK], U32, name="%s_%d_%d" % (name, c, half), align_bytes=64)
+            source = words.rearrange("g p n t -> p g (n t)")[
+                :, g0 : g0 + PAIR, PACK * BANK * c : PACK * BANK * (c + 1)
+            ]
             nc.sync.dma_start(out=chunk[:].bitcast(I32), in_=source.bitcast(I32))
             return chunk
 
-        h_rows = [load_rows(h_prev, b, "h_rows") for b in range(ROW_TILES)]
-        load_planes(0, w_last_scales)
-        w_last = [load_chunk(w_last_words, c, "w_last_%d" % c) for c in range(2)]
-        x_rows = [load_rows(x, b, "x_rows") for b in range(2)]
-        w_last += [load_chunk(w_last_words, c, "w_last_%d" % c) for c in range(2, CHUNKS)]
-        x_rows += [load_rows(x, b, "x_rows") for b in range(2, ROW_TILES)]
-        load_planes(1, w_out_scales)
-        w_out = [load_chunk(w_out_words, c, "w_out_%d" % c) for c in range(CHUNKS)]
+        h_rows, x_rows, w_last, w_out = {}, {}, {}, {}
+        h_rows[0] = load_rows(h_prev, 0, "h_rows")
+        load_planes(planes_last, w_last_scales)
+        h_rows[1] = load_rows(h_prev, 1, "h_rows")
+        h_rows[2] = load_rows(h_prev, 2, "h_rows")
+        w_last[(0, 0)] = load_chunk_half(w_last_words, 0, 0, "w_last")
+        h_rows[3] = load_rows(h_prev, 3, "h_rows")
+        w_last[(0, 1)] = load_chunk_half(w_last_words, 0, 1, "w_last")
+        x_rows[0] = load_rows(x, 0, "x_rows")
+        for half in range(2):
+            w_last[(1, half)] = load_chunk_half(w_last_words, 1, half, "w_last")
+        x_rows[1] = load_rows(x, 1, "x_rows")
+        for c in range(2, CHUNKS):
+            for half in range(2):
+                w_last[(c, half)] = load_chunk_half(w_last_words, c, half, "w_last")
+        x_rows[2] = load_rows(x, 2, "x_rows")
+        x_rows[3] = load_rows(x, 3, "x_rows")
+        load_planes(planes_out, w_out_scales)
+        for c in range(CHUNKS):
+            for half in range(2):
+                w_out[(c, half)] = load_chunk_half(w_out_words, c, half, "w_out")
+
+        half_b_last = keep.tile([P, FEATURES], BF16)
+        b_out_all = keep.tile([P, FEATURES], BF16)
+        spread = {}
+
+        def spread_bias(i):
+            spread[i] = psum.tile([P, 2 * BANK], BF16, name="spread", tag="bank")
+            for j in range(2):
+                row = 2 * i + j
+                nc.tensor.matmul(
+                    out=spread[i][:, j * BANK : (j + 1) * BANK],
+                    lhsT=ident_bf16[:, row : row + 1].to_broadcast([P, P]),
+                    rhs=bias_rows[:],
+                    start=True,
+                    stop=True,
+                )
+
+        def keep_b_last(i):
+            nc.scalar.mul(half_b_last[:, 2 * i * BANK : 2 * (i + 1) * BANK], spread[i][:], 0.5)
+
+        def keep_b_out(i):
+            nc.scalar.copy(out=b_out_all[:, 2 * i * BANK : 2 * (i + 1) * BANK], in_=spread[2 + i][:])
 
         h_words = keep.tile([P, ROW_TILES, PASSES, P], U32, align_bytes=64)
         h_scales = keep.tile([P, ROW_TILES, PASSES, P], U8, align_bytes=64)
-        for b in range(ROW_TILES):
-            grouped = stage.tile([P, PASSES, P, PACK], BF16, name="grouped_h", align_bytes=64)
+        turned_h, grouped_h = {}, {}
+
+        def turn_h(b):
             pairs = h_rows[b][:].bitcast(F32)
-            for gp in range(PASSES // 2):
-                turned = psum.tile([P, 2, 2, P], F32, name="turned_h", tag="bank")
+            for gp in range(2):
+                turned_h[(b, gp)] = psum.tile([P, 2, 2, P], F32, name="turned_h", tag="bank")
                 for gl in range(2):
                     g = 2 * gp + gl
                     for u in range(2):
                         nc.tensor.transpose(
-                            turned[:, gl, u, :], pairs[:, 256 * g + u : 256 * (g + 1) : 2], ident_f32[:]
+                            turned_h[(b, gp)][:, gl, u, :], pairs[:, 256 * g + u : 256 * (g + 1) : 2], ident_f32[:]
                         )
-                nc.scalar.copy(
-                    out=grouped[:, 2 * gp : 2 * gp + 2, :, :].bitcast(F32),
-                    in_=turned[:].rearrange("p g u r -> p g r u"),
-                )
+
+        def group_h(b, gp, copy):
+            if b not in grouped_h:
+                grouped_h[b] = stage.tile([P, PASSES, P, PACK], BF16, name="grouped_h", align_bytes=64)
+            copy(
+                out=grouped_h[b][:, 2 * gp : 2 * gp + 2, :, :].bitcast(F32),
+                in_=turned_h[(b, gp)][:].rearrange("p g u r -> p g r u"),
+            )
+
+        def quantise_h(b):
             nc.vector.quantize_mx(
                 out=h_words[:, b, :, :].rearrange("p g r -> p (g r)").bitcast(FP8X4),
                 scales=h_scales[:, b, :, :].rearrange("p g r -> p (g r)"),
-                in_=grouped[:].rearrange("p g r t -> p (g r t)"),
+                in_=grouped_h[b][:].rearrange("p g r t -> p (g r t)"),
             )
 
-        half_b_last = keep.tile([P, FEATURES], BF16)
-        b_out_all = keep.tile([P, FEATURES], BF16)
-        for w, (target, factor) in enumerate(((half_b_last, 0.5), (b_out_all, 1.0))):
-            for i in range(FEATURES // (2 * BANK)):
-                spread = psum.tile([P, 2 * BANK], BF16, name="spread", tag="bank")
-                for j in range(2):
-                    nc.tensor.matmul(
-                        out=spread[:, j * BANK : (j + 1) * BANK],
-                        lhsT=ones[:],
-                        rhs=bias_rows[:, w, (2 * i + j) * BANK : (2 * i + j + 1) * BANK],
-                        start=True,
-                        stop=True,
-                    )
-                nc.scalar.mul(target[:, 2 * i * BANK : 2 * (i + 1) * BANK], spread[:], factor)
-
-        half_inter = {}
+        half_sum, half_inter = {}, {}
         half_sums = {}
         z_rows = {}
+        accs = {}
         z_words = keep.tile([P, PAIR, PASSES, PAIR * P], U32, align_bytes=64)
         z_scales = keep.tile([P, PAIR, PASSES, PAIR * P], U8, align_bytes=64)
+        grouped_z, turned_z = {}, {}
 
-        def interactions(b):
-            half_sum = keep.tile([P, 1], F32, name="half_sum_%d" % b)
+        def row_sum(b):
+            half_sum[b] = keep.tile([P, 1], F32, name="half_sum_%d" % b)
             half_inter[b] = wide_pool.tile([P, FEATURES], F32, name="half_inter", tag="wide")
             nc.scalar.activation(
-                out=half_inter[b][:], in_=x_rows[b][:], func=ACT.Copy, scale=0.5, accum_out=half_sum[:]
+                out=half_inter[b][:],
+                in_=x_rows[b][:],
+                func=ACT.Copy,
+                scale=0.5,
+                accum_out=half_sum[b][:],
             )
-            if b < PAIR:
+
+        def interactions(b, on_vector):
+            if on_vector:
                 nc.vector.tensor_scalar(
                     out=half_inter[b][:],
                     in0=x_rows[b][:],
-                    scalar1=half_sum[:, 0:1],
+                    scalar1=half_sum[b][:, 0:1],
                     scalar2=0.0,
                     op0=ALU.mult,
                     op1=ALU.max,
                 )
             else:
-                nc.scalar.activation(out=half_inter[b][:], in_=x_rows[b][:], func=ACT.Relu, scale=half_sum[:, 0:1])
+                nc.scalar.activation(out=half_inter[b][:], in_=x_rows[b][:], func=ACT.Relu, scale=half_sum[b][:, 0:1])
+
+        def layer_1(b, c, g0, g1):
+            if g0 == 0:
+                accs[(1, b, c)] = psum.tile([P, BANK], F32, name="acc", tag="bank")
+            for g in range(g0, g1):
+                nc.tensor.matmul_mx(
+                    out=accs[(1, b, c)][:],
+                    lhsT=h_words[:, b, g, :].bitcast(FP8X4),
+                    lhsT_scale=h_scales[:, b, g, :],
+                    rhs=w_last[(c, g // PAIR)][:, g % PAIR, :].bitcast(FP8X4),
+                    rhs_scale=planes_last[4 * g : P, c * BANK : (c + 1) * BANK],
+                    start=(g == 0),
+                    stop=(g == PASSES - 1),
+                )
+
+        def keep_sum(b, c):
+            half_sums[(b, c)] = sums_pool.tile([P, BANK], F32, name="half_sums")
+            nc.vector.scalar_tensor_tensor(
+                out=half_sums[(b, c)][:],
+                in0=accs[(1, b, c)][:],
+                scalar=0.5,
+                in1=half_b_last[:, c * BANK : (c + 1) * BANK],
+                op0=ALU.mult,
+                op1=ALU.add,
+            )
 
         def finish_z(b, c):
             if b not in z_rows:
-                z_rows[b] = rows_pool.tile([P, CHUNKS, PACK, P], BF16, name="z_rows", tag="h_rows")
+                z_rows[b] = rows_pool.tile([P, FEATURES], BF16, name="z_rows", tag="h_rows")
             nc.vector.scalar_tensor_tensor(
-                out=z_rows[b][:, c, :, :].rearrange("r t p -> r p t"),
-                in0=half_sums[(b, c)][:].rearrange("r (p t) -> r p t", t=PACK),
+                out=z_rows[b][:, c * BANK : (c + 1) * BANK],
+                in0=half_sums[(b, c)][:],
                 scalar=0.0,
-                in1=half_inter[b][:, c * BANK : (c + 1) * BANK].rearrange("r (p t) -> r p t", t=PACK),
+                in1=half_inter[b][:, c * BANK : (c + 1) * BANK],
                 op0=ALU.max,
                 op1=ALU.add,
             )
 
-        def unit_banks(half, pair):
-            return [(PAIR * half + bl, PAIR * pair + cl) for bl in range(PAIR) for cl in range(PAIR)]
+        def turn_z(half, pair):
+            for cl in range(PAIR):
+                c = PAIR * pair + cl
+                turned = psum.tile([P, PAIR, 2, P], F32, name="turned_z", tag="bank")
+                turned_z[(half, c)] = turned
+                for bl in range(PAIR):
+                    pairs = z_rows[PAIR * half + bl][:].bitcast(F32)
+                    for u in range(2):
+                        nc.tensor.transpose(turned[:, bl, u, :], pairs[:, 2 * P * c + u : 2 * P * (c + 1) : 2], ident_f32[:])
 
-        def first_layer(half, pair, owed):
-            for i, (b, c) in enumerate(unit_banks(half, pair)):
-                acc = psum.tile([P, BANK], F32, name="acc", tag="bank")
-                for g in range(PASSES):
-                    nc.tensor.matmul_mx(
-                        out=acc[:],
-                        lhsT=h_words[:, b, g, :].bitcast(FP8X4),
-                        lhsT_scale=h_scales[:, b, g, :],
-                        rhs=w_last[c][:, g, :].bitcast(FP8X4),
-                        rhs_scale=planes[4 * g : P, 0, c * BANK : (c + 1) * BANK],
-                        start=(g == 0),
-                        stop=(g == PASSES - 1),
-                    )
-                half_sums[(b, c)] = sums_pool.tile([P, BANK], F32, name="half_sums")
-                nc.vector.scalar_tensor_tensor(
-                    out=half_sums[(b, c)][:],
-                    in0=acc[:],
-                    scalar=0.5,
-                    in1=half_b_last[:, c * BANK : (c + 1) * BANK],
-                    op0=ALU.mult,
-                    op1=ALU.add,
+        def group_z(half, pair):
+            grouped = stage.tile([P, PAIR, PAIR * P, PACK], BF16, name="grouped_z", align_bytes=64)
+            grouped_z[(half, pair)] = grouped
+            for cl in range(PAIR):
+                nc.scalar.copy(
+                    out=grouped[:, cl, :, :].rearrange("p (b r) t -> p b (r t)", b=PAIR).bitcast(F32).rearrange("p b (r u) -> p b r u", u=2),
+                    in_=turned_z[(half, PAIR * pair + cl)][:].rearrange("p b u r -> p b r u"),
                 )
-                if owed:
-                    finish_z(*owed[i])
 
         def quantise_z(half, pair):
-            grouped = stage.tile([P, PAIR, PAIR * P, PACK], BF16, name="grouped_z", align_bytes=64)
-            for cl in range(PAIR):
-                turned = psum.tile([P, PAIR, PACK, P], BF16, name="turned_z", tag="bank")
-                for bl in range(PAIR):
-                    for t in range(PACK):
-                        nc.tensor.transpose(
-                            turned[:, bl, t, :], z_rows[PAIR * half + bl][:, PAIR * pair + cl, t, :], ident_bf16[:]
-                        )
-                nc.scalar.copy(
-                    out=grouped[:, cl, :, :].rearrange("p (b r) t -> p b r t", b=PAIR),
-                    in_=turned[:].rearrange("p b t r -> p b r t"),
-                )
             nc.vector.quantize_mx(
                 out=z_words[:, half, PAIR * pair : PAIR * (pair + 1), :].rearrange("p g r -> p (g r)").bitcast(FP8X4),
                 scales=z_scales[:, half, PAIR * pair : PAIR * (pair + 1), :].rearrange("p g r -> p (g r)"),
-                in_=grouped[:].rearrange("p g r t -> p (g r t)"),
+                in_=grouped_z[(half, pair)][:].rearrange("p g r t -> p (g r t)"),
             )
 
-        def second_layer(half, pair, owed):
-            banks = unit_banks(half, pair)
-            accs = {}
-            for bank in banks:
-                accs[bank] = psum.tile([P, BANK], F32, name="acc", tag="bank")
-            for piece in range(PAIR):
-                for b, c in banks:
-                    for g in range(PAIR * piece, PAIR * (piece + 1)):
-                        bl = b - PAIR * half
-                        nc.tensor.matmul_mx(
-                            out=accs[(b, c)][:],
-                            lhsT=z_words[:, half, g, bl * P : (bl + 1) * P].bitcast(FP8X4),
-                            lhsT_scale=z_scales[:, half, g, bl * P : (bl + 1) * P],
-                            rhs=w_out[c][:, g, :].bitcast(FP8X4),
-                            rhs_scale=planes[4 * g : P, 1, c * BANK : (c + 1) * BANK],
-                            start=(g == 0),
-                            stop=(g == PASSES - 1),
-                        )
-            for bl in range(PAIR):
-                b = PAIR * half + bl
-                result = results.tile([P, PAIR * BANK], F32, name="result")
-                for cl in range(PAIR):
-                    c = PAIR * pair + cl
-                    nc.vector.tensor_tensor(
-                        out=result[:, cl * BANK : (cl + 1) * BANK],
-                        in0=accs[(b, c)][:],
-                        in1=b_out_all[:, c * BANK : (c + 1) * BANK],
-                        op=ALU.add,
-                    )
-                    if owed:
-                        finish_z(*owed[PAIR * bl + cl])
-                nc.sync.dma_start(
-                    out=out[b * P : (b + 1) * P, PAIR * pair * BANK : PAIR * (pair + 1) * BANK], in_=result[:]
+        def layer_2(b, c, g0, g1):
+            half, bl = b // PAIR, b % PAIR
+            if g0 == 0:
+                accs[(2, b, c)] = psum.tile([P, BANK], F32, name="acc", tag="bank")
+            for g in range(g0, g1):
+                nc.tensor.matmul_mx(
+                    out=accs[(2, b, c)][:],
+                    lhsT=z_words[:, half, g, bl * P : (bl + 1) * P].bitcast(FP8X4),
+                    lhsT_scale=z_scales[:, half, g, bl * P : (bl + 1) * P],
+                    rhs=w_out[(c, g // PAIR)][:, g % PAIR, :].bitcast(FP8X4),
+                    rhs_scale=planes_out[4 * g : P, c * BANK : (c + 1) * BANK],
+                    start=(g == 0),
+                    stop=(g == PASSES - 1),
                 )
 
-        first_layer(0, 0, [])
-        first_layer(1, 0, [])
-        interactions(0)
-        interactions(1)
-        first_layer(0, 1, unit_banks(0, 0))
+        def finish_out(b, c):
+            cols = slice(c * BANK, (c + 1) * BANK)
+            result = results.tile([P, BANK], F32, name="result")
+            nc.vector.tensor_tensor(out=result[:], in0=accs[(2, b, c)][:], in1=b_out_all[:, cols], op=ALU.add)
+            nc.sync.dma_start(out=out[b * P : (b + 1) * P, cols], in_=result[:])
+
+        scalar_copy, vector_copy = nc.scalar.copy, nc.vector.tensor_copy
+        for b in range(3):
+            turn_h(b)
+            group_h(b, 0, scalar_copy)
+            group_h(b, 1, vector_copy)
+            if b < 2:
+                spread_bias(b)
+                keep_b_last(b)
+            else:
+                spread_bias(2)
+                spread_bias(3)
+            quantise_h(b)
+        for b in range(3):
+            layer_1(b, 0, 0, 2)
+        keep_b_out(0)
+        keep_b_out(1)
+        turn_h(3)
+        group_h(3, 0, scalar_copy)
+        group_h(3, 1, vector_copy)
+        layer_1(0, 0, 2, 4)
+        keep_sum(0, 0)
+        quantise_h(3)
+        for b in range(1, 3):
+            layer_1(b, 0, 2, 4)
+            keep_sum(b, 0)
+        row_sum(0)
+        layer_1(3, 0, 0, 4)
+        keep_sum(3, 0)
+        interactions(0, True)
+        layer_1(0, 1, 0, 4)
+        keep_sum(0, 1)
+        finish_z(0, 0)
+        row_sum(1)
+        layer_1(1, 1, 0, 4)
+        keep_sum(1, 1)
+        finish_z(0, 1)
+        layer_1(2, 1, 0, 4)
+        keep_sum(2, 1)
+        interactions(1, True)
+        layer_1(3, 1, 0, 4)
+        keep_sum(3, 1)
+        finish_z(1, 0)
+        layer_1(0, 2, 0, 4)
+        keep_sum(0, 2)
+        finish_z(1, 1)
+        layer_1(1, 2, 0, 4)
+        keep_sum(1, 2)
+        finish_z(0, 2)
+        turn_z(0, 0)
+        group_z(0, 0)
+        layer_1(0, 3, 0, 4)
+        keep_sum(0, 3)
         quantise_z(0, 0)
-        interactions(2)
-        interactions(3)
-        first_layer(1, 1, unit_banks(0, 1))
+        finish_z(1, 2)
+        row_sum(2)
+        layer_1(1, 3, 0, 4)
+        keep_sum(1, 3)
+        finish_z(0, 3)
+        finish_z(1, 3)
+        layer_1(2, 2, 0, 4)
+        keep_sum(2, 2)
+        layer_1(3, 2, 0, 4)
+        keep_sum(3, 2)
+        turn_z(0, 1)
+        group_z(0, 1)
+        interactions(2, False)
+        row_sum(3)
+        layer_1(2, 3, 0, 4)
+        keep_sum(2, 3)
         quantise_z(0, 1)
-        second_layer(0, 0, unit_banks(1, 0))
+        layer_1(3, 3, 0, 4)
+        keep_sum(3, 3)
+        interactions(3, False)
+        for i in range(CHUNKS):
+            b, c = i % PAIR, i // PAIR
+            finish_z(2, i)
+            layer_2(b, c, 0, 4)
+            finish_out(b, c)
+        layer_2(0, 2, 0, 4)
+        finish_z(3, 0)
+        finish_z(3, 1)
+        finish_out(0, 2)
+        layer_2(1, 2, 0, 4)
+        turn_z(1, 0)
+        group_z(1, 0)
+        finish_z(3, 2)
+        finish_z(3, 3)
+        finish_out(1, 2)
         quantise_z(1, 0)
-        second_layer(0, 1, unit_banks(1, 1))
+        layer_2(0, 3, 0, 4)
+        turn_z(1, 1)
+        group_z(1, 1)
+        finish_out(0, 3)
+        layer_2(1, 3, 0, 4)
         quantise_z(1, 1)
-        second_layer(1, 0, [])
-        second_layer(1, 1, [])
+        finish_out(1, 3)
+        for b in range(2, 4):
+            for c in range(2):
+                layer_2(b, c, 0, 2)
+        for b in range(2, 4):
+            for c in range(2):
+                layer_2(b, c, 2, 4)
+                finish_out(b, c)
+        for b in range(2, 4):
+            for c in range(2, 4):
+                layer_2(b, c, 0, 4)
+                finish_out(b, c)

@@ -22,6 +22,7 @@ PASSES = FEATURES // K_PASS
 BANK = 512
 CHUNKS = FEATURES // BANK
 PAIR = 2
+SLOTS = FEATURES // PACK
 
 FLOPS = 2 * 2 * ROWS * FEATURES * FEATURES
 
@@ -98,7 +99,7 @@ def tile_deepfm_pa_kernel(
             for half in range(2):
                 w_out[(c, half)] = load_chunk_half(w_out_words, c, half, "w_out")
 
-        half_b_last = keep.tile([P, FEATURES], BF16)
+        b_last_all = keep.tile([P, CHUNKS, 2, P, 2], BF16)
         b_out_all = keep.tile([P, FEATURES], BF16)
         spread = {}
 
@@ -115,7 +116,11 @@ def tile_deepfm_pa_kernel(
                 )
 
         def keep_b_last(i):
-            nc.scalar.mul(half_b_last[:, 2 * i * BANK : 2 * (i + 1) * BANK], spread[i][:], 0.5)
+            for j in range(2):
+                nc.scalar.copy(
+                    out=b_last_all[:, 2 * i + j, :, :, :],
+                    in_=spread[i][:, j * BANK : (j + 1) * BANK].rearrange("p (q u e) -> p u q e", u=2, e=2),
+                )
 
         def keep_b_out(i):
             nc.scalar.copy(out=b_out_all[:, 2 * i * BANK : 2 * (i + 1) * BANK], in_=spread[2 + i][:])
@@ -150,8 +155,8 @@ def tile_deepfm_pa_kernel(
                 in_=grouped_h[b][:].rearrange("p g r t -> p (g r t)"),
             )
 
-        half_sum, half_inter = {}, {}
-        half_sums = {}
+        x_sum, inter = {}, {}
+        sums = {}
         z_rows = {}
         accs = {}
         z_words = keep.tile([P, PAIR, PASSES, PAIR * P], U32, align_bytes=64)
@@ -159,28 +164,28 @@ def tile_deepfm_pa_kernel(
         grouped_z, turned_z = {}, {}
 
         def row_sum(b):
-            half_sum[b] = keep.tile([P, 1], F32, name="half_sum_%d" % b)
-            half_inter[b] = wide_pool.tile([P, FEATURES], F32, name="half_inter", tag="wide")
+            x_sum[b] = keep.tile([P, 1], F32, name="x_sum_%d" % b)
+            inter[b] = wide_pool.tile([P, 2, SLOTS, 2], F32, name="inter", tag="wide")
             nc.scalar.activation(
-                out=half_inter[b][:],
+                out=inter[b][:].rearrange("p u q e -> p (u q e)"),
                 in_=x_rows[b][:],
                 func=ACT.Copy,
-                scale=0.5,
-                accum_out=half_sum[b][:],
+                accum_out=x_sum[b][:],
             )
 
         def interactions(b, on_vector):
+            source = x_rows[b][:].rearrange("p (q u e) -> p u q e", u=2, e=2)
             if on_vector:
                 nc.vector.tensor_scalar(
-                    out=half_inter[b][:],
-                    in0=x_rows[b][:],
-                    scalar1=half_sum[b][:, 0:1],
+                    out=inter[b][:],
+                    in0=source,
+                    scalar1=x_sum[b][:, 0:1],
                     scalar2=0.0,
                     op0=ALU.mult,
                     op1=ALU.max,
                 )
             else:
-                nc.scalar.activation(out=half_inter[b][:], in_=x_rows[b][:], func=ACT.Relu, scale=half_sum[b][:, 0:1])
+                nc.scalar.activation(out=inter[b][:], in_=source, func=ACT.Relu, scale=x_sum[b][:, 0:1])
 
         def layer_1(b, c, g0, g1):
             if g0 == 0:
@@ -197,24 +202,22 @@ def tile_deepfm_pa_kernel(
                 )
 
         def keep_sum(b, c):
-            half_sums[(b, c)] = sums_pool.tile([P, BANK], F32, name="half_sums")
-            nc.vector.scalar_tensor_tensor(
-                out=half_sums[(b, c)][:],
-                in0=accs[(1, b, c)][:],
-                scalar=0.5,
-                in1=half_b_last[:, c * BANK : (c + 1) * BANK],
-                op0=ALU.mult,
-                op1=ALU.add,
+            sums[(b, c)] = sums_pool.tile([P, 2, P, 2], F32, name="sums")
+            nc.vector.tensor_tensor(
+                out=sums[(b, c)][:],
+                in0=accs[(1, b, c)][:].rearrange("r (q u e) -> r u q e", u=2, e=2),
+                in1=b_last_all[:, c, :, :, :],
+                op=ALU.add,
             )
 
         def finish_z(b, c):
             if b not in z_rows:
-                z_rows[b] = rows_pool.tile([P, FEATURES], BF16, name="z_rows", tag="h_rows")
+                z_rows[b] = rows_pool.tile([P, 2, SLOTS, 2], BF16, name="z_rows", tag="h_rows")
             nc.vector.scalar_tensor_tensor(
-                out=z_rows[b][:, c * BANK : (c + 1) * BANK],
-                in0=half_sums[(b, c)][:],
+                out=z_rows[b][:, :, c * P : (c + 1) * P, :],
+                in0=sums[(b, c)][:],
                 scalar=0.0,
-                in1=half_inter[b][:, c * BANK : (c + 1) * BANK],
+                in1=inter[b][:, :, c * P : (c + 1) * P, :],
                 op0=ALU.max,
                 op1=ALU.add,
             )
@@ -225,9 +228,9 @@ def tile_deepfm_pa_kernel(
                 turned = psum.tile([P, PAIR, 2, P], F32, name="turned_z", tag="bank")
                 turned_z[(half, c)] = turned
                 for bl in range(PAIR):
-                    pairs = z_rows[PAIR * half + bl][:].bitcast(F32)
+                    pairs = z_rows[PAIR * half + bl][:].rearrange("p u q e -> p u (q e)").bitcast(F32)
                     for u in range(2):
-                        nc.tensor.transpose(turned[:, bl, u, :], pairs[:, 2 * P * c + u : 2 * P * (c + 1) : 2], ident_f32[:])
+                        nc.tensor.transpose(turned[:, bl, u, :], pairs[:, u, c * P : (c + 1) * P], ident_f32[:])
 
         def group_z(half, pair):
             grouped = stage.tile([P, PAIR, PAIR * P, PACK], BF16, name="grouped_z", align_bytes=64)
@@ -263,7 +266,9 @@ def tile_deepfm_pa_kernel(
         def finish_out(b, c):
             cols = slice(c * BANK, (c + 1) * BANK)
             result = results.tile([P, BANK], F32, name="result")
-            nc.vector.tensor_tensor(out=result[:], in0=accs[(2, b, c)][:], in1=b_out_all[:, cols], op=ALU.add)
+            nc.vector.scalar_tensor_tensor(
+                out=result[:], in0=accs[(2, b, c)][:], scalar=0.5, in1=b_out_all[:, cols], op0=ALU.mult, op1=ALU.add
+            )
             nc.sync.dma_start(out=out[b * P : (b + 1) * P, cols], in_=result[:])
 
         scalar_copy, vector_copy = nc.scalar.copy, nc.vector.tensor_copy

@@ -37,19 +37,22 @@ def tile_deepfm_pa_kernel(
         wide_pool = ctx.enter_context(tc.tile_pool(name="wide", bufs=ROW_TILES))
         sums_pool = ctx.enter_context(tc.tile_pool(name="sums", bufs=10))
         stage = ctx.enter_context(tc.tile_pool(name="stage", bufs=3))
-        results = ctx.enter_context(tc.tile_pool(name="results", bufs=4))
+        results = ctx.enter_context(tc.tile_pool(name="results", bufs=8))
         psum = ctx.enter_context(tc.psum_pool(name="psum", bufs=8))
         ctx.enter_context(tc.manual_schedule())
 
         bias_rows = keep.tile([P, BANK], BF16)
         nc.vector.memset(bias_rows[:].bitcast(I32), 0)
         nc.scalar.dma_start(out=bias_rows[0:CHUNKS, :], in_=b_last.rearrange("(c n) -> c n", c=CHUNKS))
-        nc.scalar.dma_start(out=bias_rows[CHUNKS : 2 * CHUNKS, :], in_=b_out.rearrange("(c n) -> c n", c=CHUNKS))
 
         planes_last = keep.tile([P, FEATURES], U8, align_bytes=64)
         planes_out = keep.tile([P, FEATURES], U8, align_bytes=64)
         nc.vector.memset(planes_last[:].bitcast(I32), 0)
         nc.vector.memset(planes_out[:].bitcast(I32), 0)
+
+        first = keep.tile([P, 1], BF16)
+        nc.vector.memset(first[:], 0.0)
+        nc.scalar.copy(out=first[:], in_=first[:])
 
         ident_bf16 = keep.tile([P, P], BF16)
         make_identity(nc, ident_bf16[:])
@@ -78,10 +81,9 @@ def tile_deepfm_pa_kernel(
             return chunk
 
         h_rows, x_rows, w_last, w_out = {}, {}, {}, {}
-        h_rows[0] = load_rows(h_prev, 0, "h_rows")
+        for b in range(3):
+            h_rows[b] = load_rows(h_prev, b, "h_rows")
         load_planes(planes_last, w_last_scales)
-        h_rows[1] = load_rows(h_prev, 1, "h_rows")
-        h_rows[2] = load_rows(h_prev, 2, "h_rows")
         w_last[(0, 0)] = load_chunk_half(w_last_words, 0, 0, "w_last")
         h_rows[3] = load_rows(h_prev, 3, "h_rows")
         w_last[(0, 1)] = load_chunk_half(w_last_words, 0, 1, "w_last")
@@ -89,18 +91,21 @@ def tile_deepfm_pa_kernel(
         for half in range(2):
             w_last[(1, half)] = load_chunk_half(w_last_words, 1, half, "w_last")
         x_rows[1] = load_rows(x, 1, "x_rows")
-        for c in range(2, CHUNKS):
-            for half in range(2):
-                w_last[(c, half)] = load_chunk_half(w_last_words, c, half, "w_last")
+        for half in range(2):
+            w_last[(2, half)] = load_chunk_half(w_last_words, 2, half, "w_last")
         x_rows[2] = load_rows(x, 2, "x_rows")
+        for half in range(2):
+            w_last[(3, half)] = load_chunk_half(w_last_words, 3, half, "w_last")
         x_rows[3] = load_rows(x, 3, "x_rows")
         load_planes(planes_out, w_out_scales)
+        b_out_all = keep.tile([P, FEATURES], BF16)
         for c in range(CHUNKS):
             for half in range(2):
                 w_out[(c, half)] = load_chunk_half(w_out_words, c, half, "w_out")
+            if c == 1:
+                nc.sync.dma_start(out=b_out_all[:], in_=b_out.partition_broadcast(P))
 
         b_last_all = keep.tile([P, CHUNKS, 2, P, 2], BF16)
-        b_out_all = keep.tile([P, FEATURES], BF16)
         spread = {}
 
         def spread_bias(i):
@@ -121,9 +126,6 @@ def tile_deepfm_pa_kernel(
                     out=b_last_all[:, 2 * i + j, :, :, :],
                     in_=spread[i][:, j * BANK : (j + 1) * BANK].rearrange("p (q u e) -> p u q e", u=2, e=2),
                 )
-
-        def keep_b_out(i):
-            nc.scalar.copy(out=b_out_all[:, 2 * i * BANK : 2 * (i + 1) * BANK], in_=spread[2 + i][:])
 
         h_words = keep.tile([P, ROW_TILES, PASSES, P], U32, align_bytes=64)
         h_scales = keep.tile([P, ROW_TILES, PASSES, P], U8, align_bytes=64)
@@ -274,22 +276,18 @@ def tile_deepfm_pa_kernel(
         scalar_copy, vector_copy = nc.scalar.copy, nc.vector.tensor_copy
         for b in range(3):
             turn_h(b)
-            group_h(b, 0, scalar_copy)
-            group_h(b, 1, vector_copy)
+            group_h(b, 0, vector_copy)
+            group_h(b, 1, scalar_copy)
             if b < 2:
                 spread_bias(b)
                 keep_b_last(b)
-            else:
-                spread_bias(2)
-                spread_bias(3)
             quantise_h(b)
-        for b in range(3):
-            layer_1(b, 0, 0, 2)
-        keep_b_out(0)
-        keep_b_out(1)
+        layer_1(0, 0, 0, 2)
+        layer_1(1, 0, 0, 2)
         turn_h(3)
-        group_h(3, 0, scalar_copy)
-        group_h(3, 1, vector_copy)
+        layer_1(2, 0, 0, 2)
+        group_h(3, 0, vector_copy)
+        group_h(3, 1, scalar_copy)
         layer_1(0, 0, 2, 4)
         keep_sum(0, 0)
         quantise_h(3)
@@ -299,6 +297,7 @@ def tile_deepfm_pa_kernel(
         row_sum(0)
         layer_1(3, 0, 0, 4)
         keep_sum(3, 0)
+
         interactions(0, True)
         layer_1(0, 1, 0, 4)
         keep_sum(0, 1)
@@ -309,61 +308,65 @@ def tile_deepfm_pa_kernel(
         finish_z(0, 1)
         layer_1(2, 1, 0, 4)
         keep_sum(2, 1)
-        interactions(1, True)
+        interactions(1, False)
         layer_1(3, 1, 0, 4)
         keep_sum(3, 1)
-        finish_z(1, 0)
         layer_1(0, 2, 0, 4)
         keep_sum(0, 2)
-        finish_z(1, 1)
+        finish_z(0, 2)
         layer_1(1, 2, 0, 4)
         keep_sum(1, 2)
-        finish_z(0, 2)
-        turn_z(0, 0)
-        group_z(0, 0)
+        finish_z(1, 0)
+        finish_z(1, 1)
+        row_sum(2)
+        interactions(2, False)
         layer_1(0, 3, 0, 4)
         keep_sum(0, 3)
-        quantise_z(0, 0)
         finish_z(1, 2)
-        row_sum(2)
+        finish_z(0, 3)
         layer_1(1, 3, 0, 4)
         keep_sum(1, 3)
-        finish_z(0, 3)
+        turn_z(0, 0)
+        group_z(0, 0)
         finish_z(1, 3)
+        quantise_z(0, 0)
+        row_sum(3)
         layer_1(2, 2, 0, 4)
         keep_sum(2, 2)
+        finish_z(2, 0)
         layer_1(3, 2, 0, 4)
         keep_sum(3, 2)
+        finish_z(2, 1)
         turn_z(0, 1)
         group_z(0, 1)
-        interactions(2, False)
-        row_sum(3)
+        interactions(3, False)
         layer_1(2, 3, 0, 4)
         keep_sum(2, 3)
         quantise_z(0, 1)
+        finish_z(2, 2)
         layer_1(3, 3, 0, 4)
         keep_sum(3, 3)
-        interactions(3, False)
-        for i in range(CHUNKS):
-            b, c = i % PAIR, i // PAIR
-            finish_z(2, i)
-            layer_2(b, c, 0, 4)
-            finish_out(b, c)
+        finish_z(2, 3)
+
+        for c in range(2):
+            for b in range(2):
+                layer_2(b, c, 0, 2)
+        for c in range(2):
+            for b in range(2):
+                layer_2(b, c, 2, 4)
+                finish_z(3, 2 * c + b)
+                finish_out(b, c)
         layer_2(0, 2, 0, 4)
-        finish_z(3, 0)
-        finish_z(3, 1)
         finish_out(0, 2)
-        layer_2(1, 2, 0, 4)
         turn_z(1, 0)
         group_z(1, 0)
-        finish_z(3, 2)
-        finish_z(3, 3)
-        finish_out(1, 2)
+        layer_2(1, 2, 0, 4)
         quantise_z(1, 0)
+        finish_out(1, 2)
         layer_2(0, 3, 0, 4)
+        finish_out(0, 3)
         turn_z(1, 1)
         group_z(1, 1)
-        finish_out(0, 3)
         layer_2(1, 3, 0, 4)
         quantise_z(1, 1)
         finish_out(1, 3)

@@ -288,9 +288,9 @@ def tile_deepfm_pa_kernel(
         layer_1(2, 0, 0, 2)
         group_h(3, 0, vector_copy)
         group_h(3, 1, scalar_copy)
+        quantise_h(3)
         layer_1(0, 0, 2, 4)
         keep_sum(0, 0)
-        quantise_h(3)
         for b in range(1, 3):
             layer_1(b, 0, 2, 4)
             keep_sum(b, 0)
@@ -298,7 +298,7 @@ def tile_deepfm_pa_kernel(
         layer_1(3, 0, 0, 4)
         keep_sum(3, 0)
 
-        interactions(0, True)
+        interactions(0, False)
         layer_1(0, 1, 0, 4)
         keep_sum(0, 1)
         finish_z(0, 0)
@@ -319,54 +319,59 @@ def tile_deepfm_pa_kernel(
         finish_z(1, 0)
         finish_z(1, 1)
         row_sum(2)
-        interactions(2, False)
         layer_1(0, 3, 0, 4)
         keep_sum(0, 3)
         finish_z(1, 2)
         finish_z(0, 3)
         layer_1(1, 3, 0, 4)
-        keep_sum(1, 3)
         turn_z(0, 0)
         group_z(0, 0)
+        keep_sum(1, 3)
         finish_z(1, 3)
         quantise_z(0, 0)
-        row_sum(3)
+        interactions(2, False)
         layer_1(2, 2, 0, 4)
         keep_sum(2, 2)
-        finish_z(2, 0)
         layer_1(3, 2, 0, 4)
         keep_sum(3, 2)
-        finish_z(2, 1)
+        layer_1(2, 3, 0, 4)
         turn_z(0, 1)
         group_z(0, 1)
-        interactions(3, False)
-        layer_1(2, 3, 0, 4)
+        finish_z(2, 0)
         keep_sum(2, 3)
         quantise_z(0, 1)
-        finish_z(2, 2)
+        row_sum(3)
+        interactions(3, False)
         layer_1(3, 3, 0, 4)
         keep_sum(3, 3)
-        finish_z(2, 3)
-
+        finish_z(2, 1)
         for c in range(2):
             for b in range(2):
                 layer_2(b, c, 0, 2)
+        finish_z(2, 2)
+        finish_z(2, 3)
         for c in range(2):
             for b in range(2):
                 layer_2(b, c, 2, 4)
-                finish_z(3, 2 * c + b)
-                finish_out(b, c)
+        finish_out(0, 0)
+        finish_out(1, 0)
+        finish_z(3, 0)
+        finish_z(3, 1)
+        finish_out(0, 1)
+        finish_z(3, 2)
+        finish_z(3, 3)
+        finish_out(1, 1)
         layer_2(0, 2, 0, 4)
-        finish_out(0, 2)
+        layer_2(1, 2, 0, 4)
         turn_z(1, 0)
         group_z(1, 0)
-        layer_2(1, 2, 0, 4)
+        finish_out(0, 2)
         quantise_z(1, 0)
         finish_out(1, 2)
         layer_2(0, 3, 0, 4)
-        finish_out(0, 3)
         turn_z(1, 1)
         group_z(1, 1)
+        finish_out(0, 3)
         layer_2(1, 3, 0, 4)
         quantise_z(1, 1)
         finish_out(1, 3)

@@ -35,7 +35,7 @@ def tile_deepfm_pa_kernel(
         keep = ctx.enter_context(tc.tile_pool(name="keep", bufs=1))
         rows_pool = ctx.enter_context(tc.tile_pool(name="rows", bufs=ROW_TILES))
         wide_pool = ctx.enter_context(tc.tile_pool(name="wide", bufs=ROW_TILES))
-        sums_pool = ctx.enter_context(tc.tile_pool(name="sums", bufs=10))
+        sums_pool = ctx.enter_context(tc.tile_pool(name="sums", bufs=7))
         stage = ctx.enter_context(tc.tile_pool(name="stage", bufs=3))
         results = ctx.enter_context(tc.tile_pool(name="results", bufs=8))
         psum = ctx.enter_context(tc.psum_pool(name="psum", bufs=8))
@@ -175,11 +175,12 @@ def tile_deepfm_pa_kernel(
                 accum_out=x_sum[b][:],
             )
 
-        def interactions(b, on_vector):
-            source = x_rows[b][:].rearrange("p (q u e) -> p u q e", u=2, e=2)
+        def interactions(b, pair, on_vector):
+            words = slice(pair * PAIR * P, (pair + 1) * PAIR * P)
+            source = x_rows[b][:].rearrange("p (q u e) -> p u q e", u=2, e=2)[:, :, words, :]
             if on_vector:
                 nc.vector.tensor_scalar(
-                    out=inter[b][:],
+                    out=inter[b][:, :, words, :],
                     in0=source,
                     scalar1=x_sum[b][:, 0:1],
                     scalar2=0.0,
@@ -187,7 +188,7 @@ def tile_deepfm_pa_kernel(
                     op1=ALU.max,
                 )
             else:
-                nc.scalar.activation(out=inter[b][:], in_=source, func=ACT.Relu, scale=x_sum[b][:, 0:1])
+                nc.scalar.activation(out=inter[b][:, :, words, :], in_=source, func=ACT.Relu, scale=x_sum[b][:, 0:1])
 
         def layer_1(b, c, g0, g1):
             if g0 == 0:
@@ -204,22 +205,25 @@ def tile_deepfm_pa_kernel(
                 )
 
         def keep_sum(b, c):
-            sums[(b, c)] = sums_pool.tile([P, 2, P, 2], F32, name="sums")
+            pair, cl = c // PAIR, c % PAIR
+            if cl == 0:
+                sums[(b, pair)] = sums_pool.tile([P, 2, PAIR * P, 2], F32, name="sums")
             nc.vector.tensor_tensor(
-                out=sums[(b, c)][:],
+                out=sums[(b, pair)][:, :, cl * P : (cl + 1) * P, :],
                 in0=accs[(1, b, c)][:].rearrange("r (q u e) -> r u q e", u=2, e=2),
                 in1=b_last_all[:, c, :, :, :],
                 op=ALU.add,
             )
 
-        def finish_z(b, c):
+        def finish_z(b, pair):
+            words = slice(pair * PAIR * P, (pair + 1) * PAIR * P)
             if b not in z_rows:
                 z_rows[b] = rows_pool.tile([P, 2, SLOTS, 2], BF16, name="z_rows", tag="h_rows")
             nc.vector.scalar_tensor_tensor(
-                out=z_rows[b][:, :, c * P : (c + 1) * P, :],
-                in0=sums[(b, c)][:],
+                out=z_rows[b][:, :, words, :],
+                in0=sums[(b, pair)][:],
                 scalar=0.0,
-                in1=inter[b][:, :, c * P : (c + 1) * P, :],
+                in1=inter[b][:, :, words, :],
                 op0=ALU.max,
                 op1=ALU.add,
             )
@@ -266,12 +270,33 @@ def tile_deepfm_pa_kernel(
                 )
 
         def finish_out(b, c):
-            cols = slice(c * BANK, (c + 1) * BANK)
-            result = results.tile([P, BANK], F32, name="result")
+            store(b, accs[(2, b, c)], c * BANK, BANK)
+
+        def store(b, acc, first_col, width):
+            cols = slice(first_col, first_col + width)
+            result = results.tile([P, width], F32, name="result", tag="result")
             nc.vector.scalar_tensor_tensor(
-                out=result[:], in0=accs[(2, b, c)][:], scalar=0.5, in1=b_out_all[:, cols], op0=ALU.mult, op1=ALU.add
+                out=result[:], in0=acc[:], scalar=0.5, in1=b_out_all[:, cols], op0=ALU.mult, op1=ALU.add
             )
             nc.sync.dma_start(out=out[b * P : (b + 1) * P, cols], in_=result[:])
+
+        def last_bank_in_halves(b, c):
+            half, bl = b // PAIR, b % PAIR
+            width = BANK // 2
+            for i in range(2):
+                acc = psum.tile([P, width], F32, name="acc_half", tag="bank")
+                for g in range(PASSES):
+                    cols = slice(i * width, (i + 1) * width)
+                    nc.tensor.matmul_mx(
+                        out=acc[:],
+                        lhsT=z_words[:, half, g, bl * P : (bl + 1) * P].bitcast(FP8X4),
+                        lhsT_scale=z_scales[:, half, g, bl * P : (bl + 1) * P],
+                        rhs=w_out[(c, g // PAIR)][:, g % PAIR, cols].bitcast(FP8X4),
+                        rhs_scale=planes_out[4 * g : P, c * BANK + i * width : c * BANK + (i + 1) * width],
+                        start=(g == 0),
+                        stop=(g == PASSES - 1),
+                    )
+                store(b, acc, c * BANK + i * width, width)
 
         scalar_copy, vector_copy = nc.scalar.copy, nc.vector.tensor_copy
         for b in range(3):
@@ -298,68 +323,64 @@ def tile_deepfm_pa_kernel(
         layer_1(3, 0, 0, 4)
         keep_sum(3, 0)
 
-        interactions(0, False)
+        interactions(0, 0, False)
         layer_1(0, 1, 0, 4)
         keep_sum(0, 1)
-        finish_z(0, 0)
         row_sum(1)
         layer_1(1, 1, 0, 4)
         keep_sum(1, 1)
-        finish_z(0, 1)
+        finish_z(0, 0)
         layer_1(2, 1, 0, 4)
         keep_sum(2, 1)
-        interactions(1, False)
+        interactions(1, 0, False)
+        interactions(0, 1, False)
         layer_1(3, 1, 0, 4)
         keep_sum(3, 1)
         layer_1(0, 2, 0, 4)
         keep_sum(0, 2)
-        finish_z(0, 2)
+        finish_z(1, 0)
         layer_1(1, 2, 0, 4)
         keep_sum(1, 2)
-        finish_z(1, 0)
-        finish_z(1, 1)
+        interactions(1, 1, False)
         row_sum(2)
+        layer_1(2, 2, 0, 4)
+        keep_sum(2, 2)
         layer_1(0, 3, 0, 4)
         keep_sum(0, 3)
-        finish_z(1, 2)
-        finish_z(0, 3)
+        finish_z(0, 1)
         layer_1(1, 3, 0, 4)
         turn_z(0, 0)
         group_z(0, 0)
         keep_sum(1, 3)
-        finish_z(1, 3)
+        finish_z(1, 1)
         quantise_z(0, 0)
-        interactions(2, False)
-        layer_1(2, 2, 0, 4)
-        keep_sum(2, 2)
+        interactions(2, 0, False)
         layer_1(3, 2, 0, 4)
         keep_sum(3, 2)
         layer_1(2, 3, 0, 4)
         turn_z(0, 1)
         group_z(0, 1)
-        finish_z(2, 0)
         keep_sum(2, 3)
+        finish_z(2, 0)
         quantise_z(0, 1)
+        interactions(2, 1, False)
         row_sum(3)
-        interactions(3, False)
+        interactions(3, 0, False)
+        interactions(3, 1, False)
         layer_1(3, 3, 0, 4)
         keep_sum(3, 3)
-        finish_z(2, 1)
         for c in range(2):
             for b in range(2):
                 layer_2(b, c, 0, 2)
-        finish_z(2, 2)
-        finish_z(2, 3)
+        finish_z(2, 1)
         for c in range(2):
             for b in range(2):
                 layer_2(b, c, 2, 4)
         finish_out(0, 0)
         finish_out(1, 0)
         finish_z(3, 0)
-        finish_z(3, 1)
         finish_out(0, 1)
-        finish_z(3, 2)
-        finish_z(3, 3)
+        finish_z(3, 1)
         finish_out(1, 1)
         layer_2(0, 2, 0, 4)
         layer_2(1, 2, 0, 4)
@@ -382,7 +403,7 @@ def tile_deepfm_pa_kernel(
             for c in range(2):
                 layer_2(b, c, 2, 4)
                 finish_out(b, c)
-        for b in range(2, 4):
-            for c in range(2, 4):
-                layer_2(b, c, 0, 4)
-                finish_out(b, c)
+        for b, c in ((2, 2), (2, 3), (3, 2)):
+            layer_2(b, c, 0, 4)
+            finish_out(b, c)
+        last_bank_in_halves(3, 3)

@@ -64,11 +64,12 @@ def tile_deepfm_pa_kernel(
             nc.sync.dma_start(out=tile_[:], in_=source[b * P : (b + 1) * P, :])
             return tile_
 
-        def load_planes(planes, scales):
+        def load_planes(planes, scales, c0, c1):
+            cols = slice(c0 * BANK, c1 * BANK)
             for q in range(4):
                 nc.sync.dma_start(
-                    out=planes[32 * q : 32 * q + 16, :].bitcast(I32),
-                    in_=scales[:, 4 * q : 4 * q + 4, :].bitcast(I32),
+                    out=planes[32 * q : 32 * q + 16, cols].bitcast(I32),
+                    in_=scales[:, 4 * q : 4 * q + 4, cols].bitcast(I32),
                 )
 
         def load_chunk_half(words, c, half, name):
@@ -81,15 +82,17 @@ def tile_deepfm_pa_kernel(
             return chunk
 
         h_rows, x_rows, w_last, w_out = {}, {}, {}, {}
-        for b in range(3):
-            h_rows[b] = load_rows(h_prev, b, "h_rows")
-        load_planes(planes_last, w_last_scales)
+        h_rows[0] = load_rows(h_prev, 0, "h_rows")
+        load_planes(planes_last, w_last_scales, 0, PAIR)
+        h_rows[1] = load_rows(h_prev, 1, "h_rows")
+        h_rows[2] = load_rows(h_prev, 2, "h_rows")
         w_last[(0, 0)] = load_chunk_half(w_last_words, 0, 0, "w_last")
         h_rows[3] = load_rows(h_prev, 3, "h_rows")
         w_last[(0, 1)] = load_chunk_half(w_last_words, 0, 1, "w_last")
         x_rows[0] = load_rows(x, 0, "x_rows")
         for half in range(2):
             w_last[(1, half)] = load_chunk_half(w_last_words, 1, half, "w_last")
+        load_planes(planes_last, w_last_scales, PAIR, CHUNKS)
         x_rows[1] = load_rows(x, 1, "x_rows")
         for half in range(2):
             w_last[(2, half)] = load_chunk_half(w_last_words, 2, half, "w_last")
@@ -97,7 +100,7 @@ def tile_deepfm_pa_kernel(
         for half in range(2):
             w_last[(3, half)] = load_chunk_half(w_last_words, 3, half, "w_last")
         x_rows[3] = load_rows(x, 3, "x_rows")
-        load_planes(planes_out, w_out_scales)
+        load_planes(planes_out, w_out_scales, 0, CHUNKS)
         b_out_all = keep.tile([P, FEATURES], BF16)
         for c in range(CHUNKS):
             for half in range(2):

@@ -23,6 +23,7 @@ BANK = 512
 CHUNKS = FEATURES // BANK
 PAIR = 2
 SLOTS = FEATURES // PACK
+WARM = 3
 
 FLOPS = 2 * 2 * ROWS * FEATURES * FEATURES
 
@@ -45,9 +46,16 @@ def tile_deepfm_pa_kernel(
         nc.vector.memset(bias_rows[:].bitcast(I32), 0)
         nc.scalar.dma_start(out=bias_rows[0:CHUNKS, :], in_=b_last.rearrange("(c n) -> c n", c=CHUNKS))
 
-        planes_last = keep.tile([P, FEATURES], U8, align_bytes=64)
-        planes_out = keep.tile([P, FEATURES], U8, align_bytes=64)
+        planes_last = keep.tile([P, FEATURES], U8, align_bytes=256)
+        planes_out = keep.tile([P, FEATURES], U8, align_bytes=256)
         nc.vector.memset(planes_last[:].bitcast(I32), 0)
+
+        idle = keep.tile([P, BANK], BF16)
+        nc.vector.memset(idle[:].bitcast(I32), 0)
+        warm = psum.tile([P, BANK], F32, name="warm", tag="bank")
+        for i in range(WARM):
+            nc.tensor.matmul(out=warm[:], lhsT=idle[:, 0:P], rhs=idle[:], start=True, stop=True)
+
         nc.vector.memset(planes_out[:].bitcast(I32), 0)
 
         first = keep.tile([P, 1], BF16)
@@ -74,7 +82,7 @@ def tile_deepfm_pa_kernel(
 
         def load_chunk_half(words, c, half, name):
             g0 = half * PAIR
-            chunk = keep.tile([P, PAIR, BANK], U32, name="%s_%d_%d" % (name, c, half), align_bytes=64)
+            chunk = keep.tile([P, PAIR, BANK], U32, name="%s_%d_%d" % (name, c, half), align_bytes=256)
             source = words.rearrange("g p n t -> p g (n t)")[
                 :, g0 : g0 + PAIR, PACK * BANK * c : PACK * BANK * (c + 1)
             ]
@@ -130,8 +138,8 @@ def tile_deepfm_pa_kernel(
                     in_=spread[i][:, j * BANK : (j + 1) * BANK].rearrange("p (q u e) -> p u q e", u=2, e=2),
                 )
 
-        h_words = keep.tile([P, ROW_TILES, PASSES, P], U32, align_bytes=64)
-        h_scales = keep.tile([P, ROW_TILES, PASSES, P], U8, align_bytes=64)
+        h_words = keep.tile([P, ROW_TILES, PASSES, P], U32, align_bytes=256)
+        h_scales = keep.tile([P, ROW_TILES, PASSES, P], U8, align_bytes=256)
         turned_h, grouped_h = {}, {}
 
         def turn_h(b):
@@ -164,8 +172,8 @@ def tile_deepfm_pa_kernel(
         sums = {}
         z_rows = {}
         accs = {}
-        z_words = keep.tile([P, PAIR, PASSES, PAIR * P], U32, align_bytes=64)
-        z_scales = keep.tile([P, PAIR, PASSES, PAIR * P], U8, align_bytes=64)
+        z_words = keep.tile([P, PAIR, PASSES, PAIR * P], U32, align_bytes=256)
+        z_scales = keep.tile([P, PAIR, PASSES, PAIR * P], U8, align_bytes=256)
         grouped_z, turned_z = {}, {}
 
         def row_sum(b):

from contextlib import ExitStack

import concourse.mybir as mybir
from concourse.masks import make_identity

F32 = mybir.dt.float32
BF16 = mybir.dt.bfloat16
I32 = mybir.dt.int32
U32 = mybir.dt.uint32
U8 = mybir.dt.uint8
FP8X4 = mybir.dt.float8_e4m3fn_x4
ALU = mybir.AluOpType
ACT = mybir.ActivationFunctionType

P = 128
PACK = 4
K_PASS = P * PACK
ROWS = 512
FEATURES = 2048
ROW_TILES = ROWS // P
PASSES = FEATURES // K_PASS
BANK = 512
CHUNKS = FEATURES // BANK
PAIR = 2
SLOTS = FEATURES // PACK
WARM = 3

FLOPS = 2 * 2 * ROWS * FEATURES * FEATURES


def tile_deepfm_pa_kernel(
    tc, h_prev, x, w_last_words, w_last_scales, b_last, w_out_words, w_out_scales, b_out, out
):
    nc = tc.nc
    with ExitStack() as ctx:
        keep = ctx.enter_context(tc.tile_pool(name="keep", bufs=1))
        rows_pool = ctx.enter_context(tc.tile_pool(name="rows", bufs=ROW_TILES))
        wide_pool = ctx.enter_context(tc.tile_pool(name="wide", bufs=ROW_TILES))
        sums_pool = ctx.enter_context(tc.tile_pool(name="sums", bufs=7))
        stage = ctx.enter_context(tc.tile_pool(name="stage", bufs=3))
        results = ctx.enter_context(tc.tile_pool(name="results", bufs=8))
        psum = ctx.enter_context(tc.psum_pool(name="psum", bufs=8))
        ctx.enter_context(tc.manual_schedule())

        bias_rows = keep.tile([P, BANK], BF16)
        nc.vector.memset(bias_rows[:].bitcast(I32), 0)
        nc.scalar.dma_start(out=bias_rows[0:CHUNKS, :], in_=b_last.rearrange("(c n) -> c n", c=CHUNKS))

        planes_last = keep.tile([P, FEATURES], U8, align_bytes=256)
        planes_out = keep.tile([P, FEATURES], U8, align_bytes=256)
        nc.vector.memset(planes_last[:].bitcast(I32), 0)

        idle = keep.tile([P, BANK], BF16)
        nc.vector.memset(idle[:].bitcast(I32), 0)
        warm = psum.tile([P, BANK], F32, name="warm", tag="bank")
        for i in range(WARM):
            nc.tensor.matmul(out=warm[:], lhsT=idle[:, 0:P], rhs=idle[:], start=True, stop=True)

        nc.vector.memset(planes_out[:].bitcast(I32), 0)

        first = keep.tile([P, 1], BF16)
        nc.vector.memset(first[:], 0.0)
        nc.scalar.copy(out=first[:], in_=first[:])

        ident_bf16 = keep.tile([P, P], BF16)
        make_identity(nc, ident_bf16[:])
        ident_f32 = keep.tile([P, P], F32)
        make_identity(nc, ident_f32[:])

        def load_rows(source, b, name):
            tile_ = rows_pool.tile([P, FEATURES], BF16, name=name, tag=name)
            nc.sync.dma_start(out=tile_[:], in_=source[b * P : (b + 1) * P, :])
            return tile_

        def load_planes(planes, scales, c0, c1):
            cols = slice(c0 * BANK, c1 * BANK)
            for q in range(4):
                nc.sync.dma_start(
                    out=planes[32 * q : 32 * q + 16, cols].bitcast(I32),
                    in_=scales[:, 4 * q : 4 * q + 4, cols].bitcast(I32),
                )

        def load_chunk_half(words, c, half, name):
            g0 = half * PAIR
            chunk = keep.tile([P, PAIR, BANK], U32, name="%s_%d_%d" % (name, c, half), align_bytes=256)
            source = words.rearrange("g p n t -> p g (n t)")[
                :, g0 : g0 + PAIR, PACK * BANK * c : PACK * BANK * (c + 1)
            ]
            nc.sync.dma_start(out=chunk[:].bitcast(I32), in_=source.bitcast(I32))
            return chunk

        h_rows, x_rows, w_last, w_out = {}, {}, {}, {}
        h_rows[0] = load_rows(h_prev, 0, "h_rows")
        load_planes(planes_last, w_last_scales, 0, PAIR)
        h_rows[1] = load_rows(h_prev, 1, "h_rows")
        h_rows[2] = load_rows(h_prev, 2, "h_rows")
        w_last[(0, 0)] = load_chunk_half(w_last_words, 0, 0, "w_last")
        h_rows[3] = load_rows(h_prev, 3, "h_rows")
        w_last[(0, 1)] = load_chunk_half(w_last_words, 0, 1, "w_last")
        x_rows[0] = load_rows(x, 0, "x_rows")
        for half in range(2):
            w_last[(1, half)] = load_chunk_half(w_last_words, 1, half, "w_last")
        load_planes(planes_last, w_last_scales, PAIR, CHUNKS)
        x_rows[1] = load_rows(x, 1, "x_rows")
        for half in range(2):
            w_last[(2, half)] = load_chunk_half(w_last_words, 2, half, "w_last")
        x_rows[2] = load_rows(x, 2, "x_rows")
        for half in range(2):
            w_last[(3, half)] = load_chunk_half(w_last_words, 3, half, "w_last")
        x_rows[3] = load_rows(x, 3, "x_rows")
        load_planes(planes_out, w_out_scales, 0, CHUNKS)
        b_out_all = keep.tile([P, FEATURES], BF16)
        for c in range(CHUNKS):
            for half in range(2):
                w_out[(c, half)] = load_chunk_half(w_out_words, c, half, "w_out")
            if c == 1:
                nc.sync.dma_start(out=b_out_all[:], in_=b_out.partition_broadcast(P))

        b_last_all = keep.tile([P, CHUNKS, 2, P, 2], BF16)
        spread = {}

        def spread_bias(i):
            spread[i] = psum.tile([P, 2 * BANK], BF16, name="spread", tag="bank")
            for j in range(2):
                row = 2 * i + j
                nc.tensor.matmul(
                    out=spread[i][:, j * BANK : (j + 1) * BANK],
                    lhsT=ident_bf16[:, row : row + 1].to_broadcast([P, P]),
                    rhs=bias_rows[:],
                    start=True,
                    stop=True,
                )

        def keep_b_last(i):
            for j in range(2):
                nc.scalar.copy(
                    out=b_last_all[:, 2 * i + j, :, :, :],
                    in_=spread[i][:, j * BANK : (j + 1) * BANK].rearrange("p (q u e) -> p u q e", u=2, e=2),
                )

        h_words = keep.tile([P, ROW_TILES, PASSES, P], U32, align_bytes=256)
        h_scales = keep.tile([P, ROW_TILES, PASSES, P], U8, align_bytes=256)
        turned_h, grouped_h = {}, {}

        def turn_h(b):
            pairs = h_rows[b][:].bitcast(F32)
            for gp in range(2):
                turned_h[(b, gp)] = psum.tile([P, 2, 2, P], F32, name="turned_h", tag="bank")
                for gl in range(2):
                    g = 2 * gp + gl
                    for u in range(2):
                        nc.tensor.transpose(
                            turned_h[(b, gp)][:, gl, u, :], pairs[:, 256 * g + u : 256 * (g + 1) : 2], ident_f32[:]
                        )

        def group_h(b, gp, copy):
            if b not in grouped_h:
                grouped_h[b] = stage.tile([P, PASSES, P, PACK], BF16, name="grouped_h", align_bytes=64)
            copy(
                out=grouped_h[b][:, 2 * gp : 2 * gp + 2, :, :].bitcast(F32),
                in_=turned_h[(b, gp)][:].rearrange("p g u r -> p g r u"),
            )

        def quantise_h(b):
            nc.vector.quantize_mx(
                out=h_words[:, b, :, :].rearrange("p g r -> p (g r)").bitcast(FP8X4),
                scales=h_scales[:, b, :, :].rearrange("p g r -> p (g r)"),
                in_=grouped_h[b][:].rearrange("p g r t -> p (g r t)"),
            )

        x_sum, inter = {}, {}
        sums = {}
        z_rows = {}
        accs = {}
        z_words = keep.tile([P, PAIR, PASSES, PAIR * P], U32, align_bytes=256)
        z_scales = keep.tile([P, PAIR, PASSES, PAIR * P], U8, align_bytes=256)
        grouped_z, turned_z = {}, {}

        def row_sum(b):
            x_sum[b] = keep.tile([P, 1], F32, name="x_sum_%d" % b)
            inter[b] = wide_pool.tile([P, 2, SLOTS, 2], F32, name="inter", tag="wide")
            nc.scalar.activation(
                out=inter[b][:].rearrange("p u q e -> p (u q e)"),
                in_=x_rows[b][:],
                func=ACT.Copy,
                accum_out=x_sum[b][:],
            )

        def interactions(b, pair, on_vector):
            words = slice(pair * PAIR * P, (pair + 1) * PAIR * P)
            source = x_rows[b][:].rearrange("p (q u e) -> p u q e", u=2, e=2)[:, :, words, :]
            if on_vector:
                nc.vector.tensor_scalar(
                    out=inter[b][:, :, words, :],
                    in0=source,
                    scalar1=x_sum[b][:, 0:1],
                    scalar2=0.0,
                    op0=ALU.mult,
                    op1=ALU.max,
                )
            else:
                nc.scalar.activation(out=inter[b][:, :, words, :], in_=source, func=ACT.Relu, scale=x_sum[b][:, 0:1])

        def layer_1(b, c, g0, g1):
            if g0 == 0:
                accs[(1, b, c)] = psum.tile([P, BANK], F32, name="acc", tag="bank")
            for g in range(g0, g1):
                nc.tensor.matmul_mx(
                    out=accs[(1, b, c)][:],
                    lhsT=h_words[:, b, g, :].bitcast(FP8X4),
                    lhsT_scale=h_scales[:, b, g, :],
                    rhs=w_last[(c, g // PAIR)][:, g % PAIR, :].bitcast(FP8X4),
                    rhs_scale=planes_last[4 * g : P, c * BANK : (c + 1) * BANK],
                    start=(g == 0),
                    stop=(g == PASSES - 1),
                )

        def keep_sum(b, c):
            pair, cl = c // PAIR, c % PAIR
            if cl == 0:
                sums[(b, pair)] = sums_pool.tile([P, 2, PAIR * P, 2], F32, name="sums")
            nc.vector.tensor_tensor(
                out=sums[(b, pair)][:, :, cl * P : (cl + 1) * P, :],
                in0=accs[(1, b, c)][:].rearrange("r (q u e) -> r u q e", u=2, e=2),
                in1=b_last_all[:, c, :, :, :],
                op=ALU.add,
            )

        def finish_z(b, pair):
            words = slice(pair * PAIR * P, (pair + 1) * PAIR * P)
            if b not in z_rows:
                z_rows[b] = rows_pool.tile([P, 2, SLOTS, 2], BF16, name="z_rows", tag="h_rows")
            nc.vector.scalar_tensor_tensor(
                out=z_rows[b][:, :, words, :],
                in0=sums[(b, pair)][:],
                scalar=0.0,
                in1=inter[b][:, :, words, :],
                op0=ALU.max,
                op1=ALU.add,
            )

        def turn_z(half, pair):
            for cl in range(PAIR):
                c = PAIR * pair + cl
                turned = psum.tile([P, PAIR, 2, P], F32, name="turned_z", tag="bank")
                turned_z[(half, c)] = turned
                for bl in range(PAIR):
                    pairs = z_rows[PAIR * half + bl][:].rearrange("p u q e -> p u (q e)").bitcast(F32)
                    for u in range(2):
                        nc.tensor.transpose(turned[:, bl, u, :], pairs[:, u, c * P : (c + 1) * P], ident_f32[:])

        def group_z(half, pair):
            grouped = stage.tile([P, PAIR, PAIR * P, PACK], BF16, name="grouped_z", align_bytes=64)
            grouped_z[(half, pair)] = grouped
            for cl in range(PAIR):
                nc.scalar.copy(
                    out=grouped[:, cl, :, :].rearrange("p (b r) t -> p b (r t)", b=PAIR).bitcast(F32).rearrange("p b (r u) -> p b r u", u=2),
                    in_=turned_z[(half, PAIR * pair + cl)][:].rearrange("p b u r -> p b r u"),
                )

        def quantise_z(half, pair):
            nc.vector.quantize_mx(
                out=z_words[:, half, PAIR * pair : PAIR * (pair + 1), :].rearrange("p g r -> p (g r)").bitcast(FP8X4),
                scales=z_scales[:, half, PAIR * pair : PAIR * (pair + 1), :].rearrange("p g r -> p (g r)"),
                in_=grouped_z[(half, pair)][:].rearrange("p g r t -> p (g r t)"),
            )

        def layer_2(b, c, g0, g1):
            half, bl = b // PAIR, b % PAIR
            if g0 == 0:
                accs[(2, b, c)] = psum.tile([P, BANK], F32, name="acc", tag="bank")
            for g in range(g0, g1):
                nc.tensor.matmul_mx(
                    out=accs[(2, b, c)][:],
                    lhsT=z_words[:, half, g, bl * P : (bl + 1) * P].bitcast(FP8X4),
                    lhsT_scale=z_scales[:, half, g, bl * P : (bl + 1) * P],
                    rhs=w_out[(c, g // PAIR)][:, g % PAIR, :].bitcast(FP8X4),
                    rhs_scale=planes_out[4 * g : P, c * BANK : (c + 1) * BANK],
                    start=(g == 0),
                    stop=(g == PASSES - 1),
                )

        def finish_out(b, c):
            store(b, accs[(2, b, c)], c * BANK, BANK)

        def store(b, acc, first_col, width):
            cols = slice(first_col, first_col + width)
            result = results.tile([P, width], F32, name="result", tag="result")
            nc.vector.scalar_tensor_tensor(
                out=result[:], in0=acc[:], scalar=0.5, in1=b_out_all[:, cols], op0=ALU.mult, op1=ALU.add
            )
            nc.sync.dma_start(out=out[b * P : (b + 1) * P, cols], in_=result[:])

        def last_bank_in_halves(b, c):
            half, bl = b // PAIR, b % PAIR
            width = BANK // 2
            for i in range(2):
                acc = psum.tile([P, width], F32, name="acc_half", tag="bank")
                for g in range(PASSES):
                    cols = slice(i * width, (i + 1) * width)
                    nc.tensor.matmul_mx(
                        out=acc[:],
                        lhsT=z_words[:, half, g, bl * P : (bl + 1) * P].bitcast(FP8X4),
                        lhsT_scale=z_scales[:, half, g, bl * P : (bl + 1) * P],
                        rhs=w_out[(c, g // PAIR)][:, g % PAIR, cols].bitcast(FP8X4),
                        rhs_scale=planes_out[4 * g : P, c * BANK + i * width : c * BANK + (i + 1) * width],
                        start=(g == 0),
                        stop=(g == PASSES - 1),
                    )
                store(b, acc, c * BANK + i * width, width)

        scalar_copy, vector_copy = nc.scalar.copy, nc.vector.tensor_copy
        for b in range(3):
            turn_h(b)
            group_h(b, 0, vector_copy)
            group_h(b, 1, scalar_copy)
            if b < 2:
                spread_bias(b)
                keep_b_last(b)
            quantise_h(b)
        layer_1(0, 0, 0, 2)
        layer_1(1, 0, 0, 2)
        turn_h(3)
        layer_1(2, 0, 0, 2)
        group_h(3, 0, vector_copy)
        group_h(3, 1, scalar_copy)
        quantise_h(3)
        layer_1(0, 0, 2, 4)
        keep_sum(0, 0)
        for b in range(1, 3):
            layer_1(b, 0, 2, 4)
            keep_sum(b, 0)
        row_sum(0)
        layer_1(3, 0, 0, 4)
        keep_sum(3, 0)

        interactions(0, 0, False)
        layer_1(0, 1, 0, 4)
        keep_sum(0, 1)
        row_sum(1)
        layer_1(1, 1, 0, 4)
        keep_sum(1, 1)
        finish_z(0, 0)
        layer_1(2, 1, 0, 4)
        keep_sum(2, 1)
        interactions(1, 0, False)
        interactions(0, 1, False)
        layer_1(3, 1, 0, 4)
        keep_sum(3, 1)
        layer_1(0, 2, 0, 4)
        keep_sum(0, 2)
        finish_z(1, 0)
        layer_1(1, 2, 0, 4)
        keep_sum(1, 2)
        interactions(1, 1, False)
        row_sum(2)
        layer_1(2, 2, 0, 4)
        keep_sum(2, 2)
        layer_1(0, 3, 0, 4)
        keep_sum(0, 3)
        finish_z(0, 1)
        layer_1(1, 3, 0, 4)
        turn_z(0, 0)
        group_z(0, 0)
        keep_sum(1, 3)
        finish_z(1, 1)
        quantise_z(0, 0)
        interactions(2, 0, False)
        layer_1(3, 2, 0, 4)
        keep_sum(3, 2)
        layer_1(2, 3, 0, 4)
        turn_z(0, 1)
        group_z(0, 1)
        keep_sum(2, 3)
        finish_z(2, 0)
        quantise_z(0, 1)
        interactions(2, 1, False)
        row_sum(3)
        interactions(3, 0, False)
        interactions(3, 1, False)
        layer_1(3, 3, 0, 4)
        keep_sum(3, 3)
        for c in range(2):
            for b in range(2):
                layer_2(b, c, 0, 2)
        finish_z(2, 1)
        for c in range(2):
            for b in range(2):
                layer_2(b, c, 2, 4)
        finish_out(0, 0)
        finish_out(1, 0)
        finish_z(3, 0)
        finish_out(0, 1)
        finish_z(3, 1)
        finish_out(1, 1)
        layer_2(0, 2, 0, 4)
        layer_2(1, 2, 0, 4)
        turn_z(1, 0)
        group_z(1, 0)
        finish_out(0, 2)
        quantise_z(1, 0)
        finish_out(1, 2)
        layer_2(0, 3, 0, 4)
        turn_z(1, 1)
        group_z(1, 1)
        finish_out(0, 3)
        layer_2(1, 3, 0, 4)
        quantise_z(1, 1)
        finish_out(1, 3)
        for b in range(2, 4):
            for c in range(2):
                layer_2(b, c, 0, 2)
        for b in range(2, 4):
            for c in range(2):
                layer_2(b, c, 2, 4)
                finish_out(b, c)
        for b, c in ((2, 2), (2, 3), (3, 2)):
            layer_2(b, c, 0, 4)
            finish_out(b, c)
        last_bank_in_halves(3, 3)
